import numpy as np
import ml_dtypes


def mxq(x, axis, fmt="e4m3"):
    dtype, down = {"e4m3": (ml_dtypes.float8_e4m3fn, 7), "e5m2": (ml_dtypes.float8_e5m2, 14)}[fmt]
    v = np.moveaxis(np.asarray(x, np.float32).astype(ml_dtypes.bfloat16).astype(np.float64), axis, -1)
    blocks = v.reshape(v.shape[:-1] + (-1, 32))
    amax = np.abs(blocks).max(-1, keepdims=True)
    byte = np.maximum(np.where(amax > 0, np.frexp(amax)[1] - 1 + 127, 0) - down, 1)
    scale = np.exp2(byte - 127.0)
    codes = (blocks / scale).astype(np.float32).astype(dtype).astype(np.float64)
    return np.moveaxis((codes * scale).reshape(v.shape), -1, axis)


WIDE = False


def mx_kscale(k):
    if not WIDE:
        return np.ones(k)
    levels = np.array([18, -18])
    if k % 512:
        return np.exp2(np.random.permutation(np.resize(levels, k // 32))).repeat(32)
    a = np.empty((k // 512, 16))
    for p in range(k // 512):
        a[p, :8] = np.random.permutation(np.resize(levels, 8))
        for g in range(8):
            far = levels[np.abs(levels - a[p, g]) >= 10]
            a[p, g + 8] = far[np.random.randint(len(far))]
    return np.exp2(a.ravel()).repeat(32)


BF16 = ml_dtypes.bfloat16


def bf(x):
    return np.asarray(x, np.float32).astype(BF16)


def f64(x):
    return np.asarray(x).astype(np.float64)


B, D, NS = 1024, 2048, 512


def relu(v):
    return np.maximum(v, 0.0)


def setup_inputs():
    s = mx_kscale(B)[:, None]
    u = mx_kscale(NS)
    v = mx_kscale(NS)
    x_batch = bf(np.random.uniform(size=(B, D)))
    p0 = bf(np.random.standard_normal((B, D)))
    wtd0 = bf(np.random.standard_normal((NS, D)) / np.sqrt(D))
    W_som_in = bf(np.random.standard_normal((NS, D)) * 1.5 / np.sqrt(D))
    wvs0 = bf(np.random.standard_normal((NS, NS)) / np.sqrt(NS))
    g = bf(4.0 * np.random.standard_normal((B, NS)) * np.exp2(np.random.randint(-6, 1, (B, 1))) / s * u)
    z_vip = f64(p0) @ f64(wtd0).T
    z_som = relu(f64(x_batch) @ f64(W_som_in).T) - relu(z_vip) @ f64(wvs0).T
    return {
        "x_batch": x_batch,
        "predicted": bf(f64(p0) * s),
        "W_vip_td": bf(f64(wtd0) / v[:, None]),
        "W_som_in": W_som_in,
        "W_vip_som": bf(f64(wvs0) * v[None, :] / u[:, None]),
        "z_vip": np.asarray(z_vip, np.float32),
        "z_som": np.asarray(z_som, np.float32),
        "grad_out": g,
    }


def reference(x_batch, predicted, W_vip_td, W_som_in, W_vip_som, z_vip, z_som, grad_out):
    dz2 = f64(grad_out) * (f64(z_som) > 0.0)
    dh = -(mxq(dz2, 1, "e5m2") @ mxq(f64(W_vip_som), 0, "e4m3"))
    dz1 = dh * (f64(z_vip) > 0.0)
    dpredicted = mxq(dz1, 1, "e5m2") @ mxq(f64(W_vip_td), 0, "e4m3")
    dW_vip_td = mxq(dz1, 0, "e5m2").T @ mxq(f64(predicted), 0, "e4m3")
    return dpredicted, dW_vip_td

@@ -1,0 +1,231 @@
+from contextlib import ExitStack
+
+import concourse.mybir as mybir
+from concourse.masks import make_identity
+
+B, D, NS = 1024, 2048, 512
+FLOPS = 2 * B * NS * NS + 2 * 2 * B * NS * D
+BYTES = 2 * (B * D + NS * D + NS * NS + B * NS) + 4 * 2 * B * NS + 4 * (B * D + NS * D)
+
+F32 = mybir.dt.float32
+BF16 = mybir.dt.bfloat16
+U32 = mybir.dt.uint32
+U8 = mybir.dt.uint8
+E4M3 = mybir.dt.float8_e4m3fn_x4
+E5M2 = mybir.dt.float8_e5m2_x4
+ALU = mybir.AluOpType
+
+P = 128
+PACK = 4
+K_PASS = P * PACK
+N = 512
+GROUPS = B // K_PASS
+CHUNKS = D // N
+BANKS = 8
+STAGES = 3
+
+
+def tile_pecircuits_pa_v_kernel(
+    tc, x_batch, predicted, W_vip_td, W_som_in, W_vip_som, z_vip, z_som, grad_out, out_0, out_1
+):
+    nc = tc.nc
+    with ExitStack() as ctx:
+        sb = ctx.enter_context(tc.tile_pool(name="sb", bufs=1))
+        ps = ctx.enter_context(tc.psum_pool(name="ps", bufs=1))
+        ctx.enter_context(tc.manual_schedule())
+
+        counts = {"bank": 0, "vector": 0, "scalar": 0}
+
+        def new_bank():
+            n = counts["bank"]
+            counts["bank"] = n + 1
+            return ps.tile([P, N], F32, name="bank%d" % n, tag="bank%d" % (n % BANKS))
+
+        def new_stage(engine):
+            n = counts[engine]
+            counts[engine] = n + 1
+            return sb.tile([P, PACK * N], BF16, name="stage_%s%d" % (engine, n),
+                           tag="stage_%s%d" % (engine, n % STAGES), align_bytes=64)
+
+        def load(name, src, dtype):
+            rows = src.rearrange("(p j) w -> p j w", j=PACK)
+            t = sb.tile(list(rows.shape), dtype, name=name, tag=name, align_bytes=64)
+            nc.sync.dma_start(out=t[:], in_=rows)
+            return t
+
+        def tokens(g):
+            return slice(g * K_PASS, (g + 1) * K_PASS)
+
+        half_d = D // 2
+        w_som = load("w_som", W_vip_som, BF16)
+        w_td = [load("w_td0", W_vip_td[:, :half_d], BF16)]
+        grad = [load("grad0", grad_out[tokens(0), :], BF16)]
+        zs = [load("zs0", z_som[tokens(0), :], F32)]
+        w_td.append(load("w_td1", W_vip_td[:, half_d:], BF16))
+        zv = [load("zv0", z_vip[tokens(0), :], F32)]
+        grad.append(load("grad1", grad_out[tokens(1), :], BF16))
+        zs.append(load("zs1", z_som[tokens(1), :], F32))
+        zv.append(load("zv1", z_vip[tokens(1), :], F32))
+        pred = [load("pred%d" % g, predicted[tokens(g), :], BF16) for g in range(GROUPS)]
+
+        ident = sb.tile([P, P], F32, name="ident", align_bytes=64)
+        make_identity(nc, ident[:])
+
+        def interleave(engine, src, negate=False):
+            stage = new_stage(engine)
+            dst = stage[:].rearrange("p (c i t) -> p c t i", i=4, t=PACK)
+            src = src.rearrange("p t (c i) -> p c t i", i=4)
+            if negate:
+                nc.vector.tensor_scalar(out=dst, in0=src, scalar1=-1.0, scalar2=None, op0=ALU.mult)
+            elif engine == "vector":
+                nc.vector.tensor_copy(out=dst, in_=src)
+            else:
+                nc.scalar.copy(out=dst, in_=src)
+            return stage
+
+        def quantize(name, stage, fmt):
+            codes = sb.tile([P, N], U32, name=name + "_codes", align_bytes=64)
+            scales = sb.tile([P, N], U8, name=name + "_scales", align_bytes=64)
+            nc.vector.quantize_mx(out=codes[:].bitcast(fmt), scales=scales[:], in_=stage[:])
+            return codes, scales
+
+        def matmul(bank, left, m, right, start, stop):
+            cols = slice(m * P, (m + 1) * P)
+            nc.tensor.matmul_mx(
+                out=bank[:],
+                lhsT=left[0][:, cols].bitcast(E5M2), lhsT_scale=left[1][:, cols],
+                rhs=right[0][:].bitcast(E4M3), rhs_scale=right[1][:],
+                start=start, stop=stop,
+            )
+
+        def td_chunk(c):
+            return w_td[c // 2][:, :, (c % 2) * N:(c % 2 + 1) * N]
+
+        def mask_grad(g):
+            halves = []
+            for h in range(2):
+                dz2 = sb.tile([P, 2 * NS], BF16, name="dz2_%d_%d" % (g, h), align_bytes=64)
+                nc.vector.scalar_tensor_tensor(
+                    out=dz2[:],
+                    in0=zs[g][:, 2 * h:2 * h + 2, :].rearrange("p j w -> p (j w)"), scalar=0.0,
+                    in1=grad[g][:, 2 * h:2 * h + 2, :].rearrange("p j w -> p (j w)"),
+                    op0=ALU.is_gt, op1=ALU.mult,
+                )
+                halves.append(dz2[:])
+            return halves
+
+        def turn(halves):
+            stage = new_stage("scalar")
+            stage_words = stage[:].bitcast(F32)
+            for h in range(2):
+                words = halves[h].bitcast(F32)
+                bank = new_bank()
+                for j in range(2):
+                    for u in range(2):
+                        q = 2 * j + u
+                        nc.tensor.transpose(bank[:, q * P:(q + 1) * P],
+                                            words[:, 2 * P * j + u:2 * P * (j + 1):2], ident[:])
+                nc.scalar.copy(
+                    out=stage_words[:, h * N:(h + 1) * N].rearrange("p (j r u) -> p j r u", j=2, u=2),
+                    in_=bank[:].rearrange("p (j u r) -> p j r u", j=2, u=2),
+                )
+            return stage
+
+        def back_through_som(g, dz2_q, w_som_q):
+            dz1 = sb.tile([P, PACK * NS], BF16, name="dz1_%d" % g, align_bytes=64)
+            for j in range(PACK):
+                bank = new_bank()
+                matmul(bank, dz2_q, j, w_som_q, True, True)
+                nc.vector.scalar_tensor_tensor(
+                    out=dz1[:, j * NS:(j + 1) * NS], in0=zv[g][:, j, :], scalar=0.0, in1=bank[:],
+                    op0=ALU.is_gt, op1=ALU.mult,
+                )
+            return dz1
+
+        def halves_of(dz1):
+            return [dz1[:, :2 * NS], dz1[:, 2 * NS:]]
+
+        def rows_of(dz1):
+            return dz1[:].rearrange("p (j w) -> p j w", j=PACK)
+
+        result_tags = ["res%d" % i for i in range(6)] + ["w_td0", "zs0", "w_td1", "zv0", "zs1", "zv1"]
+        counts["result"] = 0
+
+        def new_result():
+            n = counts["result"]
+            counts["result"] = n + 1
+            return sb.tile([P, D], F32, name="result%d" % n, tag=result_tags[n], align_bytes=64)
+
+        def grad_predicted(g, j, dz1_v, w_td_q):
+            res = new_result()
+            for c in range(CHUNKS):
+                bank = new_bank()
+                matmul(bank, dz1_v, j, w_td_q[c], True, True)
+                nc.scalar.copy(out=res[:, c * N:(c + 1) * N], in_=bank[:])
+            rows = out_0[tokens(g), :].rearrange("(p j) d -> p j d", j=PACK)
+            nc.sync.dma_start(out=rows[:, j, :], in_=res[:])
+
+        w_som_s = interleave("vector", w_som[:], negate=True)
+        td0_s = interleave("scalar", td_chunk(0))
+        w_som_q = quantize("w_som", w_som_s, E4M3)
+        td1_s = interleave("scalar", td_chunk(1))
+        w_td_q = [quantize("w_td_c0", td0_s, E4M3)]
+        dz2_t = turn(mask_grad(0))
+        w_td_q.append(quantize("w_td_c1", td1_s, E4M3))
+        dz2_q = quantize("dz2_0", dz2_t, E5M2)
+        td3_s = interleave("scalar", td_chunk(3))
+        td2_s = interleave("vector", td_chunk(2))
+        dz1 = [back_through_som(0, dz2_q, w_som_q)]
+        dz1_t = turn(halves_of(dz1[0]))
+        w_td_q.append(quantize("w_td_c2", td2_s, E4M3))
+        w_td_q.append(quantize("w_td_c3", td3_s, E4M3))
+        dz1_v = [quantize("dz1v_0", dz1_t, E5M2)]
+        grad_predicted(0, 0, dz1_v[0], w_td_q)
+
+        dz2_t = turn(mask_grad(1))
+        tok_s = interleave("vector", rows_of(dz1[0]))
+        dz2_q = quantize("dz2_1", dz2_t, E5M2)
+        dz1_tok = [quantize("dz1t_0", tok_s, E5M2)]
+        grad_predicted(0, 1, dz1_v[0], w_td_q)
+        dz1.append(back_through_som(1, dz2_q, w_som_q))
+        grad_predicted(0, 2, dz1_v[0], w_td_q)
+        dz1_t = turn(halves_of(dz1[1]))
+
+        def pred_chunk(i):
+            c, g = divmod(i, GROUPS)
+            return pred[g][:, :, c * N:(c + 1) * N]
+
+        pred_s = interleave("vector", pred_chunk(0))
+        tok_s = interleave("vector", rows_of(dz1[1]))
+        pred_q = [quantize("pred_0", pred_s, E4M3)]
+        dz1_v.append(quantize("dz1v_1", dz1_t, E5M2))
+        pred_s = interleave("vector", pred_chunk(1))
+        dz1_tok.append(quantize("dz1t_1", tok_s, E5M2))
+        for i in range(1, GROUPS * CHUNKS):
+            ready = pred_s
+            if i + 1 < GROUPS * CHUNKS:
+                pred_s = interleave("vector", pred_chunk(i + 1))
+            pred_q.append(quantize("pred_%d" % i, ready, E4M3))
+
+        grad_predicted(0, 3, dz1_v[0], w_td_q)
+        for j in range(PACK):
+            grad_predicted(1, j, dz1_v[1], w_td_q)
+
+        for h in range(2):
+            res = [new_result(), new_result()]
+            for cc in range(2):
+                c = 2 * h + cc
+                for m in range(NS // P):
+                    bank = new_bank()
+                    for g in range(GROUPS):
+                        matmul(bank, dz1_tok[g], m, pred_q[GROUPS * c + g], g == 0, g == GROUPS - 1)
+                    col = (m % 2) * half_d + cc * N
+                    dst = res[m // 2][:, col:col + N]
+                    if h == 1 and m >= 2:
+                        nc.vector.tensor_copy(out=dst, in_=bank[:])
+                    else:
+                        nc.scalar.copy(out=dst, in_=bank[:])
+            for mp in range(2):
+                rows = out_1[2 * P * mp:2 * P * (mp + 1), h * half_d:(h + 1) * half_d]
+                nc.sync.dma_start(out=rows.rearrange("(m p) d -> p m d", p=P),
+                                  in_=res[mp][:].rearrange("p (m d) -> p m d", m=2))

@@ -57,11 +57,10 @@ def tile_pecircuits_pa_v_kernel(
             return slice(g * K_PASS, (g + 1) * K_PASS)
 
         half_d = D // 2
-        w_som = load("w_som", W_vip_som, BF16)
-        w_td = [load("w_td0", W_vip_td[:, :half_d], BF16)]
         grad = [load("grad0", grad_out[tokens(0), :], BF16)]
         zs = [load("zs0", z_som[tokens(0), :], F32)]
-        w_td.append(load("w_td1", W_vip_td[:, half_d:], BF16))
+        w_som = load("w_som", W_vip_som, BF16)
+        w_td = load("w_td", W_vip_td, BF16)
         zv = [load("zv0", z_vip[tokens(0), :], F32)]
         grad.append(load("grad1", grad_out[tokens(1), :], BF16))
         zs.append(load("zs1", z_som[tokens(1), :], F32))
@@ -99,20 +98,17 @@ def tile_pecircuits_pa_v_kernel(
             )
 
         def td_chunk(c):
-            return w_td[c // 2][:, :, (c % 2) * N:(c % 2 + 1) * N]
+            return w_td[:, :, c * N:(c + 1) * N]
 
-        def mask_grad(g):
-            halves = []
-            for h in range(2):
-                dz2 = sb.tile([P, 2 * NS], BF16, name="dz2_%d_%d" % (g, h), align_bytes=64)
-                nc.vector.scalar_tensor_tensor(
-                    out=dz2[:],
-                    in0=zs[g][:, 2 * h:2 * h + 2, :].rearrange("p j w -> p (j w)"), scalar=0.0,
-                    in1=grad[g][:, 2 * h:2 * h + 2, :].rearrange("p j w -> p (j w)"),
-                    op0=ALU.is_gt, op1=ALU.mult,
-                )
-                halves.append(dz2[:])
-            return halves
+        def mask_grad(g, h):
+            dz2 = sb.tile([P, 2 * NS], BF16, name="dz2_%d_%d" % (g, h), align_bytes=64)
+            nc.vector.scalar_tensor_tensor(
+                out=dz2[:],
+                in0=zs[g][:, 2 * h:2 * h + 2, :].rearrange("p j w -> p (j w)"), scalar=0.0,
+                in1=grad[g][:, 2 * h:2 * h + 2, :].rearrange("p j w -> p (j w)"),
+                op0=ALU.is_gt, op1=ALU.mult,
+            )
+            return dz2[:]
 
         def turn(halves):
             stage = new_stage("scalar")
@@ -148,7 +144,7 @@ def tile_pecircuits_pa_v_kernel(
         def rows_of(dz1):
             return dz1[:].rearrange("p (j w) -> p j w", j=PACK)
 
-        result_tags = ["res%d" % i for i in range(6)] + ["w_td0", "zs0", "w_td1", "zv0", "zs1", "zv1"]
+        result_tags = ["res%d" % i for i in range(7)] + ["zs0", "w_td", "zv0", "zs1", "zv1"]
         counts["result"] = 0
 
         def new_result():
@@ -156,49 +152,55 @@ def tile_pecircuits_pa_v_kernel(
             counts["result"] = n + 1
             return sb.tile([P, D], F32, name="result%d" % n, tag=result_tags[n], align_bytes=64)
 
-        def grad_predicted(g, j, dz1_v, w_td_q):
-            res = new_result()
-            for c in range(CHUNKS):
+        rows_0 = {}
+
+        def grad_predicted(g, j, chunks=range(CHUNKS)):
+            if (g, j) not in rows_0:
+                rows_0[g, j] = new_result()
+            res = rows_0[g, j]
+            for c in chunks:
                 bank = new_bank()
-                matmul(bank, dz1_v, j, w_td_q[c], True, True)
+                matmul(bank, dz1_v[g], j, w_td_q[c], True, True)
                 nc.scalar.copy(out=res[:, c * N:(c + 1) * N], in_=bank[:])
-            rows = out_0[tokens(g), :].rearrange("(p j) d -> p j d", j=PACK)
-            nc.sync.dma_start(out=rows[:, j, :], in_=res[:])
-
-        w_som_s = interleave("vector", w_som[:], negate=True)
-        td0_s = interleave("scalar", td_chunk(0))
-        w_som_q = quantize("w_som", w_som_s, E4M3)
-        td1_s = interleave("scalar", td_chunk(1))
-        w_td_q = [quantize("w_td_c0", td0_s, E4M3)]
-        dz2_t = turn(mask_grad(0))
-        w_td_q.append(quantize("w_td_c1", td1_s, E4M3))
-        dz2_q = quantize("dz2_0", dz2_t, E5M2)
-        td3_s = interleave("scalar", td_chunk(3))
-        td2_s = interleave("vector", td_chunk(2))
-        dz1 = [back_through_som(0, dz2_q, w_som_q)]
-        dz1_t = turn(halves_of(dz1[0]))
-        w_td_q.append(quantize("w_td_c2", td2_s, E4M3))
-        w_td_q.append(quantize("w_td_c3", td3_s, E4M3))
-        dz1_v = [quantize("dz1v_0", dz1_t, E5M2)]
-        grad_predicted(0, 0, dz1_v[0], w_td_q)
-
-        dz2_t = turn(mask_grad(1))
-        tok_s = interleave("vector", rows_of(dz1[0]))
-        dz2_q = quantize("dz2_1", dz2_t, E5M2)
-        dz1_tok = [quantize("dz1t_0", tok_s, E5M2)]
-        grad_predicted(0, 1, dz1_v[0], w_td_q)
-        dz1.append(back_through_som(1, dz2_q, w_som_q))
-        grad_predicted(0, 2, dz1_v[0], w_td_q)
-        dz1_t = turn(halves_of(dz1[1]))
+            if CHUNKS - 1 in chunks:
+                rows = out_0[tokens(g), :].rearrange("(p j) d -> p j d", j=PACK)
+                nc.sync.dma_start(out=rows[:, j, :], in_=res[:])
 
         def pred_chunk(i):
             c, g = divmod(i, GROUPS)
             return pred[g][:, :, c * N:(c + 1) * N]
 
+        dz2_t = turn([mask_grad(0, h) for h in range(2)])
+        w_som_s = interleave("vector", w_som[:], negate=True)
+        w_som_q = quantize("w_som", w_som_s, E4M3)
+        dz2_q = quantize("dz2_0", dz2_t, E5M2)
+        td_s = [interleave("vector" if c < 2 else "scalar", td_chunk(c)) for c in range(CHUNKS)]
+        dz1 = [back_through_som(0, dz2_q, w_som_q)]
+        dz1_t = turn(halves_of(dz1[0]))
+        w_td_q = [quantize("w_td_c0", td_s[0], E4M3)]
+        dz2 = [mask_grad(1, 0)]
+        dz1_v = [quantize("dz1v_0", dz1_t, E5M2)]
+        w_td_q.append(quantize("w_td_c1", td_s[1], E4M3))
+        dz2.append(mask_grad(1, 1))
+        w_td_q.extend(quantize("w_td_c%d" % c, td_s[c], E4M3) for c in range(2, CHUNKS))
+        grad_predicted(0, 0, (0, 1))
+        grad_predicted(0, 1, (0, 1))
+
+        dz2_t = turn(dz2)
+        tok_s = interleave("vector", rows_of(dz1[0]))
+        dz2_q = quantize("dz2_1", dz2_t, E5M2)
+        dz1_tok = [quantize("dz1t_0", tok_s, E5M2)]
+        grad_predicted(0, 0, (2, 3))
+        grad_predicted(0, 1, (2, 3))
+        grad_predicted(0, 2, (0, 1))
+        dz1.append(back_through_som(1, dz2_q, w_som_q))
+        grad_predicted(0, 2, (2, 3))
+        dz1_t = turn(halves_of(dz1[1]))
+
         pred_s = interleave("vector", pred_chunk(0))
         tok_s = interleave("vector", rows_of(dz1[1]))
-        pred_q = [quantize("pred_0", pred_s, E4M3)]
         dz1_v.append(quantize("dz1v_1", dz1_t, E5M2))
+        pred_q = [quantize("pred_0", pred_s, E4M3)]
         pred_s = interleave("vector", pred_chunk(1))
         dz1_tok.append(quantize("dz1t_1", tok_s, E5M2))
         for i in range(1, GROUPS * CHUNKS):
@@ -207,25 +209,34 @@ def tile_pecircuits_pa_v_kernel(
                 pred_s = interleave("vector", pred_chunk(i + 1))
             pred_q.append(quantize("pred_%d" % i, ready, E4M3))
 
-        grad_predicted(0, 3, dz1_v[0], w_td_q)
+        grad_predicted(0, 3)
         for j in range(PACK):
-            grad_predicted(1, j, dz1_v[1], w_td_q)
+            grad_predicted(1, j)
 
-        for h in range(2):
-            res = [new_result(), new_result()]
-            for cc in range(2):
-                c = 2 * h + cc
-                for m in range(NS // P):
-                    bank = new_bank()
-                    for g in range(GROUPS):
-                        matmul(bank, dz1_tok[g], m, pred_q[GROUPS * c + g], g == 0, g == GROUPS - 1)
-                    col = (m % 2) * half_d + cc * N
-                    dst = res[m // 2][:, col:col + N]
-                    if h == 1 and m >= 2:
-                        nc.vector.tensor_copy(out=dst, in_=bank[:])
-                    else:
-                        nc.scalar.copy(out=dst, in_=bank[:])
-            for mp in range(2):
-                rows = out_1[2 * P * mp:2 * P * (mp + 1), h * half_d:(h + 1) * half_d]
-                nc.sync.dma_start(out=rows.rearrange("(m p) d -> p m d", p=P),
-                                  in_=res[mp][:].rearrange("p (m d) -> p m d", m=2))
+        def grad_weight_bank(res, m, c, engine):
+            bank = new_bank()
+            for g in range(GROUPS):
+                matmul(bank, dz1_tok[g], m, pred_q[GROUPS * c + g], g == 0, g == GROUPS - 1)
+            col = (m % 2) * half_d + (c % 2) * N
+            if engine == "vector":
+                nc.vector.tensor_copy(out=res[:, col:col + N], in_=bank[:])
+            else:
+                nc.scalar.copy(out=res[:, col:col + N], in_=bank[:])
+
+        def store_weight_rows(res, mp, h):
+            rows = out_1[2 * P * mp:2 * P * (mp + 1), h * half_d:(h + 1) * half_d]
+            nc.sync.dma_start(out=rows.rearrange("(m p) d -> p m d", p=P),
+                              in_=res[:].rearrange("p (m d) -> p m d", m=2))
+
+        for mp in range(2):
+            res = new_result()
+            for c in range(2):
+                for m in (2 * mp, 2 * mp + 1):
+                    grad_weight_bank(res, m, c, "scalar")
+            store_weight_rows(res, mp, 0)
+        res = [new_result(), new_result()]
+        for c in (2, 3):
+            for m in (0, 2, 1, 3):
+                grad_weight_bank(res[m // 2], m, c, "vector" if m < 2 else "scalar")
+        for mp in range(2):
+            store_weight_rows(res[mp], mp, 1)

@@ -23,6 +23,7 @@ GROUPS = B // K_PASS
 CHUNKS = D // N
 BANKS = 8
 STAGES = 3
+PAIRED = (0, 1, 2, 3)
 
 
 def tile_pecircuits_pa_v_kernel(
@@ -144,27 +145,26 @@ def tile_pecircuits_pa_v_kernel(
         def rows_of(dz1):
             return dz1[:].rearrange("p (j w) -> p j w", j=PACK)
 
-        result_tags = ["res%d" % i for i in range(7)] + ["zs0", "w_td", "zv0", "zs1", "zv1"]
-        counts["result"] = 0
 
-        def new_result():
-            n = counts["result"]
-            counts["result"] = n + 1
-            return sb.tile([P, D], F32, name="result%d" % n, tag=result_tags[n], align_bytes=64)
-
-        rows_0 = {}
+        pair_tags = ["pair0", "pair1", "pair2", "w_td"]
+        pairs = {}
 
         def grad_predicted(g, j, chunks=range(CHUNKS)):
-            if (g, j) not in rows_0:
-                rows_0[g, j] = new_result()
-            res = rows_0[g, j]
+            n = 2 * g + j // 2
+            if n not in pairs:
+                pairs[n] = sb.tile([P, 2 * D], F32, name="pair%d" % n, tag=pair_tags[n], align_bytes=64)
+            res = pairs[n]
             for c in chunks:
                 bank = new_bank()
                 matmul(bank, dz1_v[g], j, w_td_q[c], True, True)
-                nc.scalar.copy(out=res[:, c * N:(c + 1) * N], in_=bank[:])
+                col = (j % 2) * D + c * N
+                nc.scalar.copy(out=res[:, col:col + N], in_=bank[:])
             if CHUNKS - 1 in chunks:
-                rows = out_0[tokens(g), :].rearrange("(p j) d -> p j d", j=PACK)
-                nc.sync.dma_start(out=rows[:, j, :], in_=res[:])
+                rows = out_0[tokens(g), :].rearrange("(p j) d -> p (j d)", j=PACK)
+                if n not in PAIRED:
+                    nc.sync.dma_start(out=rows[:, j * D:(j + 1) * D], in_=res[:, (j % 2) * D:(j % 2 + 1) * D])
+                elif j % 2 == 1:
+                    nc.sync.dma_start(out=rows[:, (j - 1) * D:(j + 1) * D], in_=res[:])
 
         def pred_chunk(i):
             c, g = divmod(i, GROUPS)
@@ -213,30 +213,35 @@ def tile_pecircuits_pa_v_kernel(
         for j in range(PACK):
             grad_predicted(1, j)
 
-        def grad_weight_bank(res, m, c, engine):
+        rows_1 = [sb.tile([P, D], F32, name="rows%d" % m, tag=tag, align_bytes=64)
+                  for m, tag in enumerate(["zs0", "zv0", "zs1", "zv1"])]
+
+        def grad_weight_bank(res, col, m, c, engine):
             bank = new_bank()
             for g in range(GROUPS):
                 matmul(bank, dz1_tok[g], m, pred_q[GROUPS * c + g], g == 0, g == GROUPS - 1)
-            col = (m % 2) * half_d + (c % 2) * N
             if engine == "vector":
                 nc.vector.tensor_copy(out=res[:, col:col + N], in_=bank[:])
             else:
                 nc.scalar.copy(out=res[:, col:col + N], in_=bank[:])
 
-        def store_weight_rows(res, mp, h):
-            rows = out_1[2 * P * mp:2 * P * (mp + 1), h * half_d:(h + 1) * half_d]
+        def store_half(h):
+            rows = out_1[:2 * P, h * half_d:(h + 1) * half_d]
             nc.sync.dma_start(out=rows.rearrange("(m p) d -> p m d", p=P),
-                              in_=res[:].rearrange("p (m d) -> p m d", m=2))
+                              in_=rows_1[h][:].rearrange("p (m d) -> p m d", m=2))
 
-        for mp in range(2):
-            res = new_result()
+        for c in range(2):
+            for m in range(2):
+                grad_weight_bank(rows_1[0], m * half_d + c * N, m, c, "scalar")
+        store_half(0)
+        for m in (2, 3):
             for c in range(2):
-                for m in (2 * mp, 2 * mp + 1):
-                    grad_weight_bank(res, m, c, "scalar")
-            store_weight_rows(res, mp, 0)
-        res = [new_result(), new_result()]
+                grad_weight_bank(rows_1[m], c * N, m, c, "scalar")
         for c in (2, 3):
-            for m in (0, 2, 1, 3):
-                grad_weight_bank(res[m // 2], m, c, "vector" if m < 2 else "scalar")
-        for mp in range(2):
-            store_weight_rows(res[mp], mp, 1)
+            for m in range(2):
+                grad_weight_bank(rows_1[1], m * half_d + (c - 2) * N, m, c, "vector")
+            for m in (2, 3):
+                grad_weight_bank(rows_1[m], c * N, m, c, "scalar")
+        store_half(1)
+        for m in (2, 3):
+            nc.sync.dma_start(out=out_1[m * P:(m + 1) * P, :], in_=rows_1[m][:])

from contextlib import ExitStack

import concourse.mybir as mybir
from concourse.masks import make_identity

B, D, NS = 1024, 2048, 512
FLOPS = 2 * B * NS * NS + 2 * 2 * B * NS * D
BYTES = 2 * (B * D + NS * D + NS * NS + B * NS) + 4 * 2 * B * NS + 4 * (B * D + NS * D)

F32 = mybir.dt.float32
BF16 = mybir.dt.bfloat16
U32 = mybir.dt.uint32
U8 = mybir.dt.uint8
E4M3 = mybir.dt.float8_e4m3fn_x4
E5M2 = mybir.dt.float8_e5m2_x4
ALU = mybir.AluOpType

P = 128
PACK = 4
K_PASS = P * PACK
N = 512
GROUPS = B // K_PASS
CHUNKS = D // N
BANKS = 8
STAGES = 3
PAIRED = (0, 1, 2, 3)


def tile_pecircuits_pa_v_kernel(
    tc, x_batch, predicted, W_vip_td, W_som_in, W_vip_som, z_vip, z_som, grad_out, out_0, out_1
):
    nc = tc.nc
    with ExitStack() as ctx:
        sb = ctx.enter_context(tc.tile_pool(name="sb", bufs=1))
        ps = ctx.enter_context(tc.psum_pool(name="ps", bufs=1))
        ctx.enter_context(tc.manual_schedule())

        counts = {"bank": 0, "vector": 0, "scalar": 0}

        def new_bank():
            n = counts["bank"]
            counts["bank"] = n + 1
            return ps.tile([P, N], F32, name="bank%d" % n, tag="bank%d" % (n % BANKS))

        def new_stage(engine):
            n = counts[engine]
            counts[engine] = n + 1
            return sb.tile([P, PACK * N], BF16, name="stage_%s%d" % (engine, n),
                           tag="stage_%s%d" % (engine, n % STAGES), align_bytes=64)

        def load(name, src, dtype):
            rows = src.rearrange("(p j) w -> p j w", j=PACK)
            t = sb.tile(list(rows.shape), dtype, name=name, tag=name, align_bytes=64)
            nc.sync.dma_start(out=t[:], in_=rows)
            return t

        def tokens(g):
            return slice(g * K_PASS, (g + 1) * K_PASS)

        half_d = D // 2
        grad = [load("grad0", grad_out[tokens(0), :], BF16)]
        zs = [load("zs0", z_som[tokens(0), :], F32)]
        w_som = load("w_som", W_vip_som, BF16)
        w_td = load("w_td", W_vip_td, BF16)
        zv = [load("zv0", z_vip[tokens(0), :], F32)]
        grad.append(load("grad1", grad_out[tokens(1), :], BF16))
        zs.append(load("zs1", z_som[tokens(1), :], F32))
        zv.append(load("zv1", z_vip[tokens(1), :], F32))
        pred = [load("pred%d" % g, predicted[tokens(g), :], BF16) for g in range(GROUPS)]

        ident = sb.tile([P, P], F32, name="ident", align_bytes=64)
        make_identity(nc, ident[:])

        def interleave(engine, src, negate=False):
            stage = new_stage(engine)
            dst = stage[:].rearrange("p (c i t) -> p c t i", i=4, t=PACK)
            src = src.rearrange("p t (c i) -> p c t i", i=4)
            if negate:
                nc.vector.tensor_scalar(out=dst, in0=src, scalar1=-1.0, scalar2=None, op0=ALU.mult)
            elif engine == "vector":
                nc.vector.tensor_copy(out=dst, in_=src)
            else:
                nc.scalar.copy(out=dst, in_=src)
            return stage

        def quantize(name, stage, fmt):
            codes = sb.tile([P, N], U32, name=name + "_codes", align_bytes=64)
            scales = sb.tile([P, N], U8, name=name + "_scales", align_bytes=64)
            nc.vector.quantize_mx(out=codes[:].bitcast(fmt), scales=scales[:], in_=stage[:])
            return codes, scales

        def matmul(bank, left, m, right, start, stop):
            cols = slice(m * P, (m + 1) * P)
            nc.tensor.matmul_mx(
                out=bank[:],
                lhsT=left[0][:, cols].bitcast(E5M2), lhsT_scale=left[1][:, cols],
                rhs=right[0][:].bitcast(E4M3), rhs_scale=right[1][:],
                start=start, stop=stop,
            )

        def td_chunk(c):
            return w_td[:, :, c * N:(c + 1) * N]

        def mask_grad(g, h):
            dz2 = sb.tile([P, 2 * NS], BF16, name="dz2_%d_%d" % (g, h), align_bytes=64)
            nc.vector.scalar_tensor_tensor(
                out=dz2[:],
                in0=zs[g][:, 2 * h:2 * h + 2, :].rearrange("p j w -> p (j w)"), scalar=0.0,
                in1=grad[g][:, 2 * h:2 * h + 2, :].rearrange("p j w -> p (j w)"),
                op0=ALU.is_gt, op1=ALU.mult,
            )
            return dz2[:]

        def turn(halves):
            stage = new_stage("scalar")
            stage_words = stage[:].bitcast(F32)
            for h in range(2):
                words = halves[h].bitcast(F32)
                bank = new_bank()
                for j in range(2):
                    for u in range(2):
                        q = 2 * j + u
                        nc.tensor.transpose(bank[:, q * P:(q + 1) * P],
                                            words[:, 2 * P * j + u:2 * P * (j + 1):2], ident[:])
                nc.scalar.copy(
                    out=stage_words[:, h * N:(h + 1) * N].rearrange("p (j r u) -> p j r u", j=2, u=2),
                    in_=bank[:].rearrange("p (j u r) -> p j r u", j=2, u=2),
                )
            return stage

        def back_through_som(g, dz2_q, w_som_q):
            dz1 = sb.tile([P, PACK * NS], BF16, name="dz1_%d" % g, align_bytes=64)
            for j in range(PACK):
                bank = new_bank()
                matmul(bank, dz2_q, j, w_som_q, True, True)
                nc.vector.scalar_tensor_tensor(
                    out=dz1[:, j * NS:(j + 1) * NS], in0=zv[g][:, j, :], scalar=0.0, in1=bank[:],
                    op0=ALU.is_gt, op1=ALU.mult,
                )
            return dz1

        def halves_of(dz1):
            return [dz1[:, :2 * NS], dz1[:, 2 * NS:]]

        def rows_of(dz1):
            return dz1[:].rearrange("p (j w) -> p j w", j=PACK)


        pair_tags = ["pair0", "pair1", "pair2", "w_td"]
        pairs = {}

        def grad_predicted(g, j, chunks=range(CHUNKS)):
            n = 2 * g + j // 2
            if n not in pairs:
                pairs[n] = sb.tile([P, 2 * D], F32, name="pair%d" % n, tag=pair_tags[n], align_bytes=64)
            res = pairs[n]
            for c in chunks:
                bank = new_bank()
                matmul(bank, dz1_v[g], j, w_td_q[c], True, True)
                col = (j % 2) * D + c * N
                nc.scalar.copy(out=res[:, col:col + N], in_=bank[:])
            if CHUNKS - 1 in chunks:
                rows = out_0[tokens(g), :].rearrange("(p j) d -> p (j d)", j=PACK)
                if n not in PAIRED:
                    nc.sync.dma_start(out=rows[:, j * D:(j + 1) * D], in_=res[:, (j % 2) * D:(j % 2 + 1) * D])
                elif j % 2 == 1:
                    nc.sync.dma_start(out=rows[:, (j - 1) * D:(j + 1) * D], in_=res[:])

        def pred_chunk(i):
            c, g = divmod(i, GROUPS)
            return pred[g][:, :, c * N:(c + 1) * N]

        dz2_t = turn([mask_grad(0, h) for h in range(2)])
        w_som_s = interleave("vector", w_som[:], negate=True)
        w_som_q = quantize("w_som", w_som_s, E4M3)
        dz2_q = quantize("dz2_0", dz2_t, E5M2)
        td_s = [interleave("vector" if c < 2 else "scalar", td_chunk(c)) for c in range(CHUNKS)]
        dz1 = [back_through_som(0, dz2_q, w_som_q)]
        dz1_t = turn(halves_of(dz1[0]))
        w_td_q = [quantize("w_td_c0", td_s[0], E4M3)]
        dz2 = [mask_grad(1, 0)]
        dz1_v = [quantize("dz1v_0", dz1_t, E5M2)]
        w_td_q.append(quantize("w_td_c1", td_s[1], E4M3))
        dz2.append(mask_grad(1, 1))
        w_td_q.extend(quantize("w_td_c%d" % c, td_s[c], E4M3) for c in range(2, CHUNKS))
        grad_predicted(0, 0, (0, 1))
        grad_predicted(0, 1, (0, 1))

        dz2_t = turn(dz2)
        tok_s = interleave("vector", rows_of(dz1[0]))
        dz2_q = quantize("dz2_1", dz2_t, E5M2)
        dz1_tok = [quantize("dz1t_0", tok_s, E5M2)]
        grad_predicted(0, 0, (2, 3))
        grad_predicted(0, 1, (2, 3))
        grad_predicted(0, 2, (0, 1))
        dz1.append(back_through_som(1, dz2_q, w_som_q))
        grad_predicted(0, 2, (2, 3))
        dz1_t = turn(halves_of(dz1[1]))

        pred_s = interleave("vector", pred_chunk(0))
        tok_s = interleave("vector", rows_of(dz1[1]))
        dz1_v.append(quantize("dz1v_1", dz1_t, E5M2))
        pred_q = [quantize("pred_0", pred_s, E4M3)]
        pred_s = interleave("vector", pred_chunk(1))
        dz1_tok.append(quantize("dz1t_1", tok_s, E5M2))
        for i in range(1, GROUPS * CHUNKS):
            ready = pred_s
            if i + 1 < GROUPS * CHUNKS:
                pred_s = interleave("vector", pred_chunk(i + 1))
            pred_q.append(quantize("pred_%d" % i, ready, E4M3))

        grad_predicted(0, 3)
        for j in range(PACK):
            grad_predicted(1, j)

        rows_1 = [sb.tile([P, D], F32, name="rows%d" % m, tag=tag, align_bytes=64)
                  for m, tag in enumerate(["zs0", "zv0", "zs1", "zv1"])]

        def grad_weight_bank(res, col, m, c, engine):
            bank = new_bank()
            for g in range(GROUPS):
                matmul(bank, dz1_tok[g], m, pred_q[GROUPS * c + g], g == 0, g == GROUPS - 1)
            if engine == "vector":
                nc.vector.tensor_copy(out=res[:, col:col + N], in_=bank[:])
            else:
                nc.scalar.copy(out=res[:, col:col + N], in_=bank[:])

        def store_half(h):
            rows = out_1[:2 * P, h * half_d:(h + 1) * half_d]
            nc.sync.dma_start(out=rows.rearrange("(m p) d -> p m d", p=P),
                              in_=rows_1[h][:].rearrange("p (m d) -> p m d", m=2))

        for c in range(2):
            for m in range(2):
                grad_weight_bank(rows_1[0], m * half_d + c * N, m, c, "scalar")
        store_half(0)
        for m in (2, 3):
            for c in range(2):
                grad_weight_bank(rows_1[m], c * N, m, c, "scalar")
        for c in (2, 3):
            for m in range(2):
                grad_weight_bank(rows_1[1], m * half_d + (c - 2) * N, m, c, "vector")
            for m in (2, 3):
                grad_weight_bank(rows_1[m], c * N, m, c, "scalar")
        store_half(1)
        for m in (2, 3):
            nc.sync.dma_start(out=out_1[m * P:(m + 1) * P, :], in_=rows_1[m][:])
